import numpy as np
import ml_dtypes


def mxq(x, axis, fmt="e4m3"):
    dtype, down = {"e4m3": (ml_dtypes.float8_e4m3fn, 7), "e5m2": (ml_dtypes.float8_e5m2, 14)}[fmt]
    v = np.moveaxis(np.asarray(x, np.float32).astype(ml_dtypes.bfloat16).astype(np.float64), axis, -1)
    blocks = v.reshape(v.shape[:-1] + (-1, 32))
    amax = np.abs(blocks).max(-1, keepdims=True)
    byte = np.maximum(np.where(amax > 0, np.frexp(amax)[1] - 1 + 127, 0) - down, 1)
    scale = np.exp2(byte - 127.0)
    codes = (blocks / scale).astype(np.float32).astype(dtype).astype(np.float64)
    return np.moveaxis((codes * scale).reshape(v.shape), -1, axis)


WIDE = False


def mx_kscale(k):
    if not WIDE:
        return np.ones(k)
    levels = np.array([10, -10, 5, -5, 0])
    a = np.random.permutation(np.resize(levels, k // 512 * 4)).reshape(k // 512, 4)
    idx = np.arange(k)
    return np.exp2(a[idx // 512, idx % 128 // 32])


BF16 = ml_dtypes.bfloat16


def bf(x):
    return np.asarray(x, np.float32).astype(BF16)


def f64(x):
    return np.asarray(x).astype(np.float64)


B, P, K, D, L, C0, C1, C2, C3 = 2048, 64, 128, 512, 4, 256, 512, 1024, 2048
C = C3
F = 2 * C
EPS = 1e-5


def layernorm(x, g, b):
    m = x.mean(axis=-1, keepdims=True)
    v = x.var(axis=-1, keepdims=True)
    return (x - m) / np.sqrt(v + EPS) * g + b


def l2norm(x):
    n = np.sqrt((x * x).sum(axis=-1, keepdims=True))
    return x / np.maximum(n, 1e-12)


def setup_inputs():
    s = mx_kscale(F)
    return {"pooled": bf(0.5 + 2.0 * np.random.standard_normal((B, C))),
            "proto": bf(np.random.standard_normal((1, C)) + np.random.standard_normal((P, C))),
            "ln_g": bf((1.0 + 0.1 * np.random.standard_normal(F)) * s),
            "ln_b": bf(0.1 * np.random.standard_normal(F) * s),
            "W": bf(np.random.standard_normal((F, D)) / np.sqrt(F) / s[:, None]),
            "b": bf(0.1 * np.random.standard_normal(D))}


def reference(pooled, proto, ln_g, ln_b, W, b):
    pl = f64(pooled)
    proto_ctx = np.broadcast_to(f64(proto).mean(axis=0, keepdims=True), pl.shape)
    fused = np.concatenate([pl, proto_ctx], axis=1)
    z = layernorm(fused, f64(ln_g), f64(ln_b))
    h = np.maximum((mxq(z, 1, "e4m3") @ mxq(f64(W), 0, "e4m3")) + f64(b), 0.0)
    return l2norm(h)

@@ -1,0 +1,248 @@
+from contextlib import ExitStack
+
+import concourse.mybir as mybir
+from concourse.masks import make_identity
+
+F32 = mybir.dt.float32
+BF16 = mybir.dt.bfloat16
+U32 = mybir.dt.uint32
+U8 = mybir.dt.uint8
+FP8X4 = mybir.dt.float8_e4m3fn_x4
+ACT = mybir.ActivationFunctionType
+ALU = mybir.AluOpType
+
+P = 128
+PACK = 4
+K_PASS = P * PACK
+ROWS = 2048
+CHANNELS = 2048
+PROTOS = 64
+FUSED = 2 * CHANNELS
+D_OUT = 512
+EPS = 1e-5
+TINY_NORM = 1e-12
+
+PASSES = FUSED // K_PASS
+CHUNKS = FUSED // P
+GROUP_TILES = 4
+GROUP_ROWS = GROUP_TILES * P
+GROUPS = ROWS // GROUP_ROWS
+ROW_TILES = ROWS // P
+STAT_WIDTH = 512
+STATS_PER_HALF = CHANNELS // STAT_WIDTH
+SLAB = 1024
+SLAB_PASSES = SLAB // K_PASS
+SLABS = FUSED // SLAB
+
+FLOPS = 2 * ROWS * FUSED * D_OUT
+
+
+def regroup_and_quantise(nc, planes, grouped, codes, scales):
+    nc.vector.tensor_copy(
+        out=grouped[:].rearrange("p (c i) t -> p c t i", i=4),
+        in_=planes[:].rearrange("p t (c i) -> p c t i", i=4),
+    )
+    nc.vector.quantize_mx(
+        out=codes.bitcast(FP8X4),
+        scales=scales,
+        in_=grouped[:].rearrange("p w t -> p (w t)"),
+    )
+
+
+def tile_textguidedcamfusion_pa_kernel(tc, pooled, proto, ln_g, ln_b, W, b, out):
+    nc = tc.nc
+    with ExitStack() as stack:
+        const = stack.enter_context(tc.tile_pool(name="const", bufs=1))
+        x_pool = stack.enter_context(tc.tile_pool(name="x", bufs=2 * GROUP_TILES))
+        w_stage = stack.enter_context(tc.tile_pool(name="w_stage", bufs=2))
+        y_pool = stack.enter_context(tc.tile_pool(name="y", bufs=3))
+        z_stage = stack.enter_context(tc.tile_pool(name="z_stage", bufs=3))
+        z_words = stack.enter_context(tc.tile_pool(name="z_words", bufs=4))
+        small = stack.enter_context(tc.tile_pool(name="small", bufs=2))
+        tail = stack.enter_context(tc.tile_pool(name="tail", bufs=GROUP_TILES))
+        flip_psum = stack.enter_context(tc.psum_pool(name="flip_psum", bufs=4))
+        acc_psum = stack.enter_context(tc.psum_pool(name="acc_psum", bufs=GROUP_TILES))
+
+        x_tiles = {}
+
+        def load_group(s):
+            for rt in range(s * GROUP_TILES, (s + 1) * GROUP_TILES):
+                x_tile = x_pool.tile([P, CHANNELS], BF16, name="x_tile")
+                nc.sync.dma_start(out=x_tile[:], in_=pooled[rt * P : (rt + 1) * P, :])
+                x_tiles[rt] = x_tile
+
+        load_group(0)
+
+        gain_shift_rows = const.tile([P, P], BF16)
+        nc.vector.memset(gain_shift_rows[:], 0.0)
+        nc.scalar.dma_start(out=gain_shift_rows[0:CHUNKS, :], in_=ln_g.rearrange("(c p) -> c p", p=P))
+        nc.scalar.dma_start(
+            out=gain_shift_rows[CHUNKS : 2 * CHUNKS, :], in_=ln_b.rearrange("(c p) -> c p", p=P)
+        )
+        proto_rows = const.tile([P, CHANNELS], BF16)
+        nc.vector.memset(proto_rows[PROTOS:P, :], 0.0)
+        nc.scalar.dma_start(out=proto_rows[0:PROTOS, :], in_=proto)
+        bias_rows = const.tile([P, D_OUT], BF16)
+        nc.scalar.dma_start(out=bias_rows[:], in_=b.partition_broadcast(P))
+
+        w_view = W.rearrange("(g t p) n -> g p t n", t=PACK, p=P)
+        w_planes = []
+        for g in range(PASSES):
+            w_plane = w_stage.tile([P, PACK, D_OUT], BF16, name="w_plane", bufs=PASSES)
+            nc.sync.dma_start(out=w_plane[:], in_=w_view[g])
+            w_planes.append(w_plane)
+        load_group(1)
+
+        identity = const.tile([P, P], F32)
+        make_identity(nc, identity[:])
+        ones = const.tile([P, P], BF16)
+        nc.vector.memset(ones[:], 1.0)
+        eps = const.tile([P, 1], F32)
+        nc.vector.memset(eps[:], EPS)
+
+        gain_shift_f32 = const.tile([P, P], F32)
+        nc.vector.tensor_copy(out=gain_shift_f32[:], in_=gain_shift_rows[:])
+        gain_shift_bank = flip_psum.tile([P, GROUP_ROWS], F32, name="bank")
+        nc.tensor.transpose(gain_shift_bank[:, 0:P], gain_shift_f32[:], identity[:])
+        gain_shift = const.tile([P, 2 * CHUNKS], F32)
+        nc.vector.tensor_copy(out=gain_shift[:], in_=gain_shift_bank[:, 0 : 2 * CHUNKS])
+
+        context = const.tile([P, CHANNELS], F32)
+        context_stats = const.tile([P, STATS_PER_HALF, 6], F32)
+        for j in range(STATS_PER_HALF):
+            cols = slice(j * STAT_WIDTH, (j + 1) * STAT_WIDTH)
+            sum_bank = flip_psum.tile([P, GROUP_ROWS], F32, name="bank")
+            nc.tensor.matmul(sum_bank[:], lhsT=ones[:], rhs=proto_rows[:, cols], start=True, stop=True)
+            nc.scalar.activation(out=context[:, cols], in_=sum_bank[:], func=ACT.Copy, scale=1.0 / PROTOS)
+            nc.vector.bn_stats(out=context_stats[:, j, :], in_=context[:, cols])
+
+        stats = const.tile([P, ROW_TILES, 2 * STATS_PER_HALF, 6], F32)
+        nc.vector.tensor_copy(
+            out=stats[:, :, STATS_PER_HALF:, :],
+            in_=context_stats[:].unsqueeze(1).to_broadcast([P, ROW_TILES, STATS_PER_HALF, 6]),
+        )
+
+        w_codes = const.tile([P, PASSES, D_OUT], U32, align_bytes=64)
+        w_scales = const.tile([P, PASSES, D_OUT], U8, align_bytes=64)
+
+        def quantise_w(g):
+            w_grouped = w_stage.tile([P, D_OUT, PACK], BF16, align_bytes=64, name="w_grouped")
+            regroup_and_quantise(nc, w_planes[g], w_grouped, w_codes[:, g, :], w_scales[:, g, :])
+
+        def row_statistics(s):
+            mean_var = small.tile([P, GROUP_TILES, 2], F32, name="mean_var")
+            for r in range(GROUP_TILES):
+                rt = s * GROUP_TILES + r
+                for j in range(STATS_PER_HALF):
+                    cols = slice(j * STAT_WIDTH, (j + 1) * STAT_WIDTH)
+                    nc.vector.bn_stats(out=stats[:, rt, j, :], in_=x_tiles[rt][:, cols])
+                nc.vector.bn_aggr(
+                    out=mean_var[:, r, :], in_=stats[:, rt, :, :].rearrange("p j v -> p (j v)")
+                )
+            rstd = small.tile([P, GROUP_TILES], F32, name="rstd")
+            nc.scalar.activation(out=rstd[:], in_=mean_var[:, :, 1], func=ACT.Sqrt, bias=eps[:])
+            nc.vector.reciprocal(out=rstd[:], in_=rstd[:])
+            return mean_var, rstd
+
+        def normalise(s, slab, mean_var, rstd):
+            y = y_pool.tile([P, GROUP_TILES, SLAB], F32, name="y")
+            for r in range(GROUP_TILES):
+                first = slab * SLAB
+                if first < CHANNELS:
+                    source = x_tiles[s * GROUP_TILES + r][:, first : first + SLAB]
+                else:
+                    source = context[:, first - CHANNELS : first - CHANNELS + SLAB]
+                nc.vector.tensor_scalar(
+                    out=y[:, r, :],
+                    in0=source,
+                    scalar1=mean_var[:, r, 0:1],
+                    scalar2=rstd[:, r : r + 1],
+                    op0=ALU.subtract,
+                    op1=ALU.mult,
+                )
+            return y
+
+        def flip_and_quantise(g, y):
+            z_planes = z_stage.tile([P, PACK, GROUP_ROWS], BF16, name="z_planes")
+            for t in range(PACK):
+                c = g * PACK + t
+                first = (c * P) % SLAB
+                bank = flip_psum.tile([P, GROUP_ROWS], F32, name="bank")
+                for r in range(GROUP_TILES):
+                    nc.tensor.transpose(
+                        bank[:, r * P : (r + 1) * P], y[:, r, first : first + P], identity[:]
+                    )
+                nc.scalar.activation(
+                    out=z_planes[:, t, :],
+                    in_=bank[:],
+                    func=ACT.Identity,
+                    scale=gain_shift[:, c : c + 1],
+                    bias=gain_shift[:, CHUNKS + c : CHUNKS + c + 1],
+                )
+            z_grouped = z_stage.tile([P, GROUP_ROWS, PACK], BF16, align_bytes=64, name="z_grouped")
+            z_codes = z_words.tile([P, GROUP_ROWS], U32, align_bytes=64, name="z_codes")
+            z_scales = z_words.tile([P, GROUP_ROWS], U8, align_bytes=64, name="z_scales")
+            regroup_and_quantise(nc, z_planes, z_grouped, z_codes[:], z_scales[:])
+            return z_codes, z_scales
+
+        def multiply(g, z_codes, z_scales, accs):
+            for r in range(GROUP_TILES):
+                rows = slice(r * P, (r + 1) * P)
+                nc.tensor.matmul_mx(
+                    out=accs[r][:],
+                    lhsT=z_codes[:, rows].bitcast(FP8X4),
+                    lhsT_scale=z_scales[:, rows],
+                    rhs=w_codes[:, g, :].bitcast(FP8X4),
+                    rhs_scale=w_scales[:, g, :],
+                    start=(g == 0),
+                    stop=(g == PASSES - 1),
+                )
+
+        def finish(s, accs):
+            square_sum = small.tile([P, GROUP_TILES], F32, name="square_sum")
+            biased = []
+            for r in range(GROUP_TILES):
+                h = tail.tile([P, D_OUT], F32, name="h", bufs=2 * GROUP_TILES)
+                nc.vector.tensor_tensor(out=h[:], in0=accs[r][:], in1=bias_rows[:], op=ALU.add)
+                squares = tail.tile([P, D_OUT], F32, name="squares", bufs=2)
+                nc.vector.scalar_tensor_tensor(
+                    out=squares[:],
+                    in0=h[:],
+                    scalar=0.0,
+                    in1=h[:],
+                    op0=ALU.max,
+                    op1=ALU.mult,
+                    accum_out=square_sum[:, r : r + 1],
+                )
+                biased.append(h)
+            inverse_norm = small.tile([P, GROUP_TILES], F32, name="inverse_norm")
+            nc.scalar.activation(out=inverse_norm[:], in_=square_sum[:], func=ACT.Sqrt)
+            nc.vector.tensor_scalar_max(out=inverse_norm[:], in0=inverse_norm[:], scalar1=TINY_NORM)
+            nc.vector.reciprocal(out=inverse_norm[:], in_=inverse_norm[:])
+            for r in range(GROUP_TILES):
+                rt = s * GROUP_TILES + r
+                unit = tail.tile([P, D_OUT], F32, name="unit")
+                nc.scalar.activation(
+                    out=unit[:], in_=biased[r][:], func=ACT.Relu, scale=inverse_norm[:, r : r + 1]
+                )
+                nc.sync.dma_start(out=out[rt * P : (rt + 1) * P, :], in_=unit[:])
+
+        group_stats = row_statistics(0)
+        for s in range(GROUPS):
+            mean_var, rstd = group_stats
+            accs = []
+            for r in range(GROUP_TILES):
+                acc = acc_psum.tile([P, D_OUT], F32, name="acc")
+                accs.append(acc)
+            for slab in range(SLABS):
+                y = normalise(s, slab, mean_var, rstd)
+                for g in range(slab * SLAB_PASSES, (slab + 1) * SLAB_PASSES):
+                    z_codes, z_scales = flip_and_quantise(g, y)
+                    if s == 0:
+                        quantise_w(g)
+                    multiply(g, z_codes, z_scales, accs)
+                if slab == 1 and s + 1 < GROUPS:
+                    group_stats = row_statistics(s + 1)
+                if slab == 1 and s + 2 < GROUPS:
+                    load_group(s + 2)
+            finish(s, accs)

@@ -33,12 +33,13 @@ STATS_PER_HALF = CHANNELS // STAT_WIDTH
 SLAB = 1024
 SLAB_PASSES = SLAB // K_PASS
 SLABS = FUSED // SLAB
+W_AHEAD = 4
 
 FLOPS = 2 * ROWS * FUSED * D_OUT
 
 
-def regroup_and_quantise(nc, planes, grouped, codes, scales):
-    nc.vector.tensor_copy(
+def regroup_and_quantise(nc, copy, planes, grouped, codes, scales):
+    copy(
         out=grouped[:].rearrange("p (c i) t -> p c t i", i=4),
         in_=planes[:].rearrange("p t (c i) -> p c t i", i=4),
     )
@@ -55,7 +56,7 @@ def tile_textguidedcamfusion_pa_kernel(tc, pooled, proto, ln_g, ln_b, W, b, out)
         const = stack.enter_context(tc.tile_pool(name="const", bufs=1))
         x_pool = stack.enter_context(tc.tile_pool(name="x", bufs=2 * GROUP_TILES))
         w_stage = stack.enter_context(tc.tile_pool(name="w_stage", bufs=2))
-        y_pool = stack.enter_context(tc.tile_pool(name="y", bufs=3))
+        y_pool = stack.enter_context(tc.tile_pool(name="y", bufs=2))
         z_stage = stack.enter_context(tc.tile_pool(name="z_stage", bufs=3))
         z_words = stack.enter_context(tc.tile_pool(name="z_words", bufs=4))
         small = stack.enter_context(tc.tile_pool(name="small", bufs=2))
@@ -86,11 +87,15 @@ def tile_textguidedcamfusion_pa_kernel(tc, pooled, proto, ln_g, ln_b, W, b, out)
         nc.scalar.dma_start(out=bias_rows[:], in_=b.partition_broadcast(P))
 
         w_view = W.rearrange("(g t p) n -> g p t n", t=PACK, p=P)
-        w_planes = []
-        for g in range(PASSES):
-            w_plane = w_stage.tile([P, PACK, D_OUT], BF16, name="w_plane", bufs=PASSES)
+        w_planes = {}
+
+        def load_w(g):
+            w_plane = w_stage.tile([P, PACK, D_OUT], BF16, name="w_plane", bufs=W_AHEAD)
             nc.sync.dma_start(out=w_plane[:], in_=w_view[g])
-            w_planes.append(w_plane)
+            w_planes[g] = w_plane
+
+        for g in range(W_AHEAD):
+            load_w(g)
         load_group(1)
 
         identity = const.tile([P, P], F32)
@@ -127,7 +132,11 @@ def tile_textguidedcamfusion_pa_kernel(tc, pooled, proto, ln_g, ln_b, W, b, out)
 
         def quantise_w(g):
             w_grouped = w_stage.tile([P, D_OUT, PACK], BF16, align_bytes=64, name="w_grouped")
-            regroup_and_quantise(nc, w_planes[g], w_grouped, w_codes[:, g, :], w_scales[:, g, :])
+            regroup_and_quantise(
+                nc, nc.scalar.copy, w_planes[g], w_grouped, w_codes[:, g, :], w_scales[:, g, :]
+            )
+            if g + W_AHEAD < PASSES:
+                load_w(g + W_AHEAD)
 
         def row_statistics(s):
             mean_var = small.tile([P, GROUP_TILES, 2], F32, name="mean_var")
@@ -142,22 +151,29 @@ def tile_textguidedcamfusion_pa_kernel(tc, pooled, proto, ln_g, ln_b, W, b, out)
             rstd = small.tile([P, GROUP_TILES], F32, name="rstd")
             nc.scalar.activation(out=rstd[:], in_=mean_var[:, :, 1], func=ACT.Sqrt, bias=eps[:])
             nc.vector.reciprocal(out=rstd[:], in_=rstd[:])
-            return mean_var, rstd
+            neg_mean = small.tile([P, GROUP_TILES], F32, name="neg_mean")
+            nc.vector.tensor_scalar_mul(out=neg_mean[:], in0=mean_var[:, :, 0], scalar1=-1.0)
+            return neg_mean, rstd
 
-        def normalise(s, slab, mean_var, rstd):
-            y = y_pool.tile([P, GROUP_TILES, SLAB], F32, name="y")
+        def normalise(s, slab, neg_mean, rstd):
+            first = slab * SLAB
+            if first < CHANNELS:
+                y = y_pool.tile([P, GROUP_TILES, SLAB], F32, name="y_pooled")
+            else:
+                y = y_pool.tile([P, GROUP_TILES, SLAB], F32, name="y_context")
             for r in range(GROUP_TILES):
-                first = slab * SLAB
                 if first < CHANNELS:
+                    engine = nc.vector
                     source = x_tiles[s * GROUP_TILES + r][:, first : first + SLAB]
                 else:
+                    engine = nc.gpsimd
                     source = context[:, first - CHANNELS : first - CHANNELS + SLAB]
-                nc.vector.tensor_scalar(
+                engine.tensor_scalar(
                     out=y[:, r, :],
                     in0=source,
-                    scalar1=mean_var[:, r, 0:1],
+                    scalar1=neg_mean[:, r : r + 1],
                     scalar2=rstd[:, r : r + 1],
-                    op0=ALU.subtract,
+                    op0=ALU.add,
                     op1=ALU.mult,
                 )
             return y
@@ -182,7 +198,7 @@ def tile_textguidedcamfusion_pa_kernel(tc, pooled, proto, ln_g, ln_b, W, b, out)
             z_grouped = z_stage.tile([P, GROUP_ROWS, PACK], BF16, align_bytes=64, name="z_grouped")
             z_codes = z_words.tile([P, GROUP_ROWS], U32, align_bytes=64, name="z_codes")
             z_scales = z_words.tile([P, GROUP_ROWS], U8, align_bytes=64, name="z_scales")
-            regroup_and_quantise(nc, z_planes, z_grouped, z_codes[:], z_scales[:])
+            regroup_and_quantise(nc, nc.vector.tensor_copy, z_planes, z_grouped, z_codes[:], z_scales[:])
             return z_codes, z_scales
 
         def multiply(g, z_codes, z_scales, accs):
@@ -200,42 +216,43 @@ def tile_textguidedcamfusion_pa_kernel(tc, pooled, proto, ln_g, ln_b, W, b, out)
 
         def finish(s, accs):
             square_sum = small.tile([P, GROUP_TILES], F32, name="square_sum")
-            biased = []
+            hs = []
             for r in range(GROUP_TILES):
                 h = tail.tile([P, D_OUT], F32, name="h", bufs=2 * GROUP_TILES)
                 nc.vector.tensor_tensor(out=h[:], in0=accs[r][:], in1=bias_rows[:], op=ALU.add)
+                hs.append(h)
+            for r in range(GROUP_TILES):
+                nc.scalar.activation(out=hs[r][:], in_=hs[r][:], func=ACT.Relu)
+            for r in range(GROUP_TILES):
                 squares = tail.tile([P, D_OUT], F32, name="squares", bufs=2)
-                nc.vector.scalar_tensor_tensor(
-                    out=squares[:],
-                    in0=h[:],
-                    scalar=0.0,
-                    in1=h[:],
-                    op0=ALU.max,
-                    op1=ALU.mult,
-                    accum_out=square_sum[:, r : r + 1],
+                nc.scalar.activation(
+                    out=squares[:], in_=hs[r][:], func=ACT.Square, accum_out=square_sum[:, r : r + 1]
                 )
-                biased.append(h)
             inverse_norm = small.tile([P, GROUP_TILES], F32, name="inverse_norm")
             nc.scalar.activation(out=inverse_norm[:], in_=square_sum[:], func=ACT.Sqrt)
             nc.vector.tensor_scalar_max(out=inverse_norm[:], in0=inverse_norm[:], scalar1=TINY_NORM)
             nc.vector.reciprocal(out=inverse_norm[:], in_=inverse_norm[:])
             for r in range(GROUP_TILES):
                 rt = s * GROUP_TILES + r
-                unit = tail.tile([P, D_OUT], F32, name="unit")
-                nc.scalar.activation(
-                    out=unit[:], in_=biased[r][:], func=ACT.Relu, scale=inverse_norm[:, r : r + 1]
+                nc.gpsimd.tensor_scalar(
+                    out=hs[r][:],
+                    in0=hs[r][:],
+                    scalar1=inverse_norm[:, r : r + 1],
+                    scalar2=0.0,
+                    op0=ALU.mult,
+                    op1=ALU.add,
                 )
-                nc.sync.dma_start(out=out[rt * P : (rt + 1) * P, :], in_=unit[:])
+                nc.sync.dma_start(out=out[rt * P : (rt + 1) * P, :], in_=hs[r][:])
 
         group_stats = row_statistics(0)
         for s in range(GROUPS):
-            mean_var, rstd = group_stats
+            neg_mean, rstd = group_stats
             accs = []
             for r in range(GROUP_TILES):
                 acc = acc_psum.tile([P, D_OUT], F32, name="acc")
                 accs.append(acc)
             for slab in range(SLABS):
-                y = normalise(s, slab, mean_var, rstd)
+                y = normalise(s, slab, neg_mean, rstd)
                 for g in range(slab * SLAB_PASSES, (slab + 1) * SLAB_PASSES):
                     z_codes, z_scales = flip_and_quantise(g, y)
                     if s == 0:

@@ -27,7 +27,6 @@ CHUNKS = FUSED // P
 GROUP_TILES = 4
 GROUP_ROWS = GROUP_TILES * P
 GROUPS = ROWS // GROUP_ROWS
-ROW_TILES = ROWS // P
 STAT_WIDTH = 512
 STATS_PER_HALF = CHANNELS // STAT_WIDTH
 SLAB = 1024
@@ -38,15 +37,16 @@ W_AHEAD = 4
 FLOPS = 2 * ROWS * FUSED * D_OUT
 
 
-def regroup_and_quantise(nc, copy, planes, grouped, codes, scales):
+def regroup(copy, planes, grouped):
     copy(
         out=grouped[:].rearrange("p (c i) t -> p c t i", i=4),
         in_=planes[:].rearrange("p t (c i) -> p c t i", i=4),
     )
+
+
+def quantise(nc, grouped, codes, scales):
     nc.vector.quantize_mx(
-        out=codes.bitcast(FP8X4),
-        scales=scales,
-        in_=grouped[:].rearrange("p w t -> p (w t)"),
+        out=codes.bitcast(FP8X4), scales=scales, in_=grouped[:].rearrange("p w t -> p (w t)")
     )
 
 
@@ -56,9 +56,9 @@ def tile_textguidedcamfusion_pa_kernel(tc, pooled, proto, ln_g, ln_b, W, b, out)
         const = stack.enter_context(tc.tile_pool(name="const", bufs=1))
         x_pool = stack.enter_context(tc.tile_pool(name="x", bufs=2 * GROUP_TILES))
         w_stage = stack.enter_context(tc.tile_pool(name="w_stage", bufs=2))
-        y_pool = stack.enter_context(tc.tile_pool(name="y", bufs=2))
+        y_pool = stack.enter_context(tc.tile_pool(name="y", bufs=3))
         z_stage = stack.enter_context(tc.tile_pool(name="z_stage", bufs=3))
-        z_words = stack.enter_context(tc.tile_pool(name="z_words", bufs=4))
+        z_words = stack.enter_context(tc.tile_pool(name="z_words", bufs=3))
         small = stack.enter_context(tc.tile_pool(name="small", bufs=2))
         tail = stack.enter_context(tc.tile_pool(name="tail", bufs=GROUP_TILES))
         flip_psum = stack.enter_context(tc.psum_pool(name="flip_psum", bufs=4))
@@ -121,10 +121,10 @@ def tile_textguidedcamfusion_pa_kernel(tc, pooled, proto, ln_g, ln_b, W, b, out)
             nc.scalar.activation(out=context[:, cols], in_=sum_bank[:], func=ACT.Copy, scale=1.0 / PROTOS)
             nc.vector.bn_stats(out=context_stats[:, j, :], in_=context[:, cols])
 
-        stats = const.tile([P, ROW_TILES, 2 * STATS_PER_HALF, 6], F32)
+        stats = const.tile([P, GROUPS * GROUP_TILES, 2 * STATS_PER_HALF, 6], F32)
         nc.vector.tensor_copy(
             out=stats[:, :, STATS_PER_HALF:, :],
-            in_=context_stats[:].unsqueeze(1).to_broadcast([P, ROW_TILES, STATS_PER_HALF, 6]),
+            in_=context_stats[:].unsqueeze(1).to_broadcast([P, GROUPS * GROUP_TILES, STATS_PER_HALF, 6]),
         )
 
         w_codes = const.tile([P, PASSES, D_OUT], U32, align_bytes=64)
@@ -132,11 +132,12 @@ def tile_textguidedcamfusion_pa_kernel(tc, pooled, proto, ln_g, ln_b, W, b, out)
 
         def quantise_w(g):
             w_grouped = w_stage.tile([P, D_OUT, PACK], BF16, align_bytes=64, name="w_grouped")
-            regroup_and_quantise(
-                nc, nc.scalar.copy, w_planes[g], w_grouped, w_codes[:, g, :], w_scales[:, g, :]
-            )
+            regroup(nc.scalar.copy, w_planes[g], w_grouped)
+            quantise(nc, w_grouped, w_codes[:, g, :], w_scales[:, g, :])
             if g + W_AHEAD < PASSES:
                 load_w(g + W_AHEAD)
+
+        row_scale = {}
 
         def row_statistics(s):
             mean_var = small.tile([P, GROUP_TILES, 2], F32, name="mean_var")
@@ -151,34 +152,40 @@ def tile_textguidedcamfusion_pa_kernel(tc, pooled, proto, ln_g, ln_b, W, b, out)
             rstd = small.tile([P, GROUP_TILES], F32, name="rstd")
             nc.scalar.activation(out=rstd[:], in_=mean_var[:, :, 1], func=ACT.Sqrt, bias=eps[:])
             nc.vector.reciprocal(out=rstd[:], in_=rstd[:])
-            neg_mean = small.tile([P, GROUP_TILES], F32, name="neg_mean")
-            nc.vector.tensor_scalar_mul(out=neg_mean[:], in0=mean_var[:, :, 0], scalar1=-1.0)
-            return neg_mean, rstd
+            shift = small.tile([P, GROUP_TILES], F32, name="shift")
+            nc.vector.scalar_tensor_tensor(
+                out=shift[:], in0=mean_var[:, :, 0], scalar=-1.0, in1=rstd[:], op0=ALU.mult, op1=ALU.mult
+            )
+            row_scale[s] = (rstd, shift)
 
-        def normalise(s, slab, neg_mean, rstd):
+        y_slabs = {}
+
+        def normalise(s, slab):
+            rstd, shift = row_scale[s]
             first = slab * SLAB
-            if first < CHANNELS:
-                y = y_pool.tile([P, GROUP_TILES, SLAB], F32, name="y_pooled")
-            else:
-                y = y_pool.tile([P, GROUP_TILES, SLAB], F32, name="y_context")
+            y = y_pool.tile([P, GROUP_TILES, SLAB], F32, name="y")
             for r in range(GROUP_TILES):
                 if first < CHANNELS:
-                    engine = nc.vector
-                    source = x_tiles[s * GROUP_TILES + r][:, first : first + SLAB]
+                    nc.vector.tensor_scalar(
+                        out=y[:, r, :],
+                        in0=x_tiles[s * GROUP_TILES + r][:, first : first + SLAB],
+                        scalar1=rstd[:, r : r + 1],
+                        scalar2=shift[:, r : r + 1],
+                        op0=ALU.mult,
+                        op1=ALU.add,
+                    )
                 else:
-                    engine = nc.gpsimd
-                    source = context[:, first - CHANNELS : first - CHANNELS + SLAB]
-                engine.tensor_scalar(
-                    out=y[:, r, :],
-                    in0=source,
-                    scalar1=neg_mean[:, r : r + 1],
-                    scalar2=rstd[:, r : r + 1],
-                    op0=ALU.add,
-                    op1=ALU.mult,
-                )
-            return y
+                    nc.scalar.activation(
+                        out=y[:, r, :],
+                        in_=context[:, first - CHANNELS : first - CHANNELS + SLAB],
+                        func=ACT.Identity,
+                        scale=rstd[:, r : r + 1],
+                        bias=shift[:, r : r + 1],
+                    )
+            y_slabs[(s, slab)] = y
 
-        def flip_and_quantise(g, y):
+        def flip(s, g):
+            y = y_slabs[(s, g // SLAB_PASSES)]
             z_planes = z_stage.tile([P, PACK, GROUP_ROWS], BF16, name="z_planes")
             for t in range(PACK):
                 c = g * PACK + t
@@ -196,12 +203,21 @@ def tile_textguidedcamfusion_pa_kernel(tc, pooled, proto, ln_g, ln_b, W, b, out)
                     bias=gain_shift[:, CHUNKS + c : CHUNKS + c + 1],
                 )
             z_grouped = z_stage.tile([P, GROUP_ROWS, PACK], BF16, align_bytes=64, name="z_grouped")
+            regroup(nc.vector.tensor_copy, z_planes, z_grouped)
+            return z_grouped
+
+        accs_of = {}
+
+        def multiply(s, g, z_grouped):
+            if g == 0:
+                accs_of[s] = []
+                for r in range(GROUP_TILES):
+                    acc = acc_psum.tile([P, D_OUT], F32, name="acc")
+                    accs_of[s].append(acc)
+            accs = accs_of[s]
             z_codes = z_words.tile([P, GROUP_ROWS], U32, align_bytes=64, name="z_codes")
             z_scales = z_words.tile([P, GROUP_ROWS], U8, align_bytes=64, name="z_scales")
-            regroup_and_quantise(nc, nc.vector.tensor_copy, z_planes, z_grouped, z_codes[:], z_scales[:])
-            return z_codes, z_scales
-
-        def multiply(g, z_codes, z_scales, accs):
+            quantise(nc, z_grouped, z_codes[:], z_scales[:])
             for r in range(GROUP_TILES):
                 rows = slice(r * P, (r + 1) * P)
                 nc.tensor.matmul_mx(
@@ -214,7 +230,8 @@ def tile_textguidedcamfusion_pa_kernel(tc, pooled, proto, ln_g, ln_b, W, b, out)
                     stop=(g == PASSES - 1),
                 )
 
-        def finish(s, accs):
+        def finish(s):
+            accs = accs_of[s]
             square_sum = small.tile([P, GROUP_TILES], F32, name="square_sum")
             hs = []
             for r in range(GROUP_TILES):
@@ -222,11 +239,15 @@ def tile_textguidedcamfusion_pa_kernel(tc, pooled, proto, ln_g, ln_b, W, b, out)
                 nc.vector.tensor_tensor(out=h[:], in0=accs[r][:], in1=bias_rows[:], op=ALU.add)
                 hs.append(h)
             for r in range(GROUP_TILES):
-                nc.scalar.activation(out=hs[r][:], in_=hs[r][:], func=ACT.Relu)
-            for r in range(GROUP_TILES):
                 squares = tail.tile([P, D_OUT], F32, name="squares", bufs=2)
-                nc.scalar.activation(
-                    out=squares[:], in_=hs[r][:], func=ACT.Square, accum_out=square_sum[:, r : r + 1]
+                nc.vector.scalar_tensor_tensor(
+                    out=squares[:],
+                    in0=hs[r][:],
+                    scalar=0.0,
+                    in1=hs[r][:],
+                    op0=ALU.max,
+                    op1=ALU.mult,
+                    accum_out=square_sum[:, r : r + 1],
                 )
             inverse_norm = small.tile([P, GROUP_TILES], F32, name="inverse_norm")
             nc.scalar.activation(out=inverse_norm[:], in_=square_sum[:], func=ACT.Sqrt)
@@ -234,32 +255,32 @@ def tile_textguidedcamfusion_pa_kernel(tc, pooled, proto, ln_g, ln_b, W, b, out)
             nc.vector.reciprocal(out=inverse_norm[:], in_=inverse_norm[:])
             for r in range(GROUP_TILES):
                 rt = s * GROUP_TILES + r
-                nc.gpsimd.tensor_scalar(
-                    out=hs[r][:],
-                    in0=hs[r][:],
-                    scalar1=inverse_norm[:, r : r + 1],
-                    scalar2=0.0,
-                    op0=ALU.mult,
-                    op1=ALU.add,
+                nc.scalar.activation(
+                    out=hs[r][:], in_=hs[r][:], func=ACT.Relu, scale=inverse_norm[:, r : r + 1]
                 )
                 nc.sync.dma_start(out=out[rt * P : (rt + 1) * P, :], in_=hs[r][:])
 
-        group_stats = row_statistics(0)
+        row_statistics(0)
+        normalise(0, 0)
+        waiting = None
         for s in range(GROUPS):
-            neg_mean, rstd = group_stats
-            accs = []
-            for r in range(GROUP_TILES):
-                acc = acc_psum.tile([P, D_OUT], F32, name="acc")
-                accs.append(acc)
             for slab in range(SLABS):
-                y = normalise(s, slab, neg_mean, rstd)
+                if slab + 1 < SLABS:
+                    normalise(s, slab + 1)
+                elif s + 1 < GROUPS:
+                    normalise(s + 1, 0)
+                if slab == 0 and s + 2 < GROUPS:
+                    load_group(s + 2)
+                if slab == 1 and s + 1 < GROUPS:
+                    row_statistics(s + 1)
                 for g in range(slab * SLAB_PASSES, (slab + 1) * SLAB_PASSES):
-                    z_codes, z_scales = flip_and_quantise(g, y)
+                    z_grouped = flip(s, g)
                     if s == 0:
                         quantise_w(g)
-                    multiply(g, z_codes, z_scales, accs)
-                if slab == 1 and s + 1 < GROUPS:
-                    group_stats = row_statistics(s + 1)
-                if slab == 1 and s + 2 < GROUPS:
-                    load_group(s + 2)
-            finish(s, accs)
+                    if waiting is not None:
+                        multiply(*waiting)
+                    if waiting is not None and g == 0:
+                        finish(s - 1)
+                    waiting = (s, g, z_grouped)
+        multiply(*waiting)
+        finish(GROUPS - 1)

@@ -32,6 +32,7 @@ STATS_PER_HALF = CHANNELS // STAT_WIDTH
 SLAB = 1024
 SLAB_PASSES = SLAB // K_PASS
 SLABS = FUSED // SLAB
+SLABS_AHEAD = 2
 W_AHEAD = 4
 
 FLOPS = 2 * ROWS * FUSED * D_OUT
@@ -139,16 +140,21 @@ def tile_textguidedcamfusion_pa_kernel(tc, pooled, proto, ln_g, ln_b, W, b, out)
 
         row_scale = {}
 
-        def row_statistics(s):
-            mean_var = small.tile([P, GROUP_TILES, 2], F32, name="mean_var")
-            for r in range(GROUP_TILES):
-                rt = s * GROUP_TILES + r
-                for j in range(STATS_PER_HALF):
-                    cols = slice(j * STAT_WIDTH, (j + 1) * STAT_WIDTH)
-                    nc.vector.bn_stats(out=stats[:, rt, j, :], in_=x_tiles[rt][:, cols])
-                nc.vector.bn_aggr(
-                    out=mean_var[:, r, :], in_=stats[:, rt, :, :].rearrange("p j v -> p (j v)")
-                )
+        mean_vars = {}
+
+        def tile_statistics(s, r):
+            if r == 0:
+                mean_vars[s] = small.tile([P, GROUP_TILES, 2], F32, name="mean_var")
+            rt = s * GROUP_TILES + r
+            for j in range(STATS_PER_HALF):
+                cols = slice(j * STAT_WIDTH, (j + 1) * STAT_WIDTH)
+                nc.vector.bn_stats(out=stats[:, rt, j, :], in_=x_tiles[rt][:, cols])
+            nc.vector.bn_aggr(
+                out=mean_vars[s][:, r, :], in_=stats[:, rt, :, :].rearrange("p j v -> p (j v)")
+            )
+
+        def group_scales(s):
+            mean_var = mean_vars[s]
             rstd = small.tile([P, GROUP_TILES], F32, name="rstd")
             nc.scalar.activation(out=rstd[:], in_=mean_var[:, :, 1], func=ACT.Sqrt, bias=eps[:])
             nc.vector.reciprocal(out=rstd[:], in_=rstd[:])
@@ -160,29 +166,25 @@ def tile_textguidedcamfusion_pa_kernel(tc, pooled, proto, ln_g, ln_b, W, b, out)
 
         y_slabs = {}
 
-        def normalise(s, slab):
+        def normalise(s, slab, row_tiles):
             rstd, shift = row_scale[s]
             first = slab * SLAB
-            y = y_pool.tile([P, GROUP_TILES, SLAB], F32, name="y")
-            for r in range(GROUP_TILES):
+            if row_tiles[0] == 0:
+                y_slabs[(s, slab)] = y_pool.tile([P, GROUP_TILES, SLAB], F32, name="y")
+            y = y_slabs[(s, slab)]
+            for r in row_tiles:
                 if first < CHANNELS:
-                    nc.vector.tensor_scalar(
-                        out=y[:, r, :],
-                        in0=x_tiles[s * GROUP_TILES + r][:, first : first + SLAB],
-                        scalar1=rstd[:, r : r + 1],
-                        scalar2=shift[:, r : r + 1],
-                        op0=ALU.mult,
-                        op1=ALU.add,
-                    )
+                    fused = x_tiles[s * GROUP_TILES + r][:, first : first + SLAB]
                 else:
-                    nc.scalar.activation(
-                        out=y[:, r, :],
-                        in_=context[:, first - CHANNELS : first - CHANNELS + SLAB],
-                        func=ACT.Identity,
-                        scale=rstd[:, r : r + 1],
-                        bias=shift[:, r : r + 1],
-                    )
-            y_slabs[(s, slab)] = y
+                    fused = context[:, first - CHANNELS : first - CHANNELS + SLAB]
+                nc.gpsimd.tensor_scalar(
+                    out=y[:, r, :],
+                    in0=fused,
+                    scalar1=rstd[:, r : r + 1],
+                    scalar2=shift[:, r : r + 1],
+                    op0=ALU.mult,
+                    op1=ALU.add,
+                )
 
         def flip(s, g):
             y = y_slabs[(s, g // SLAB_PASSES)]
@@ -195,15 +197,18 @@ def tile_textguidedcamfusion_pa_kernel(tc, pooled, proto, ln_g, ln_b, W, b, out)
                     nc.tensor.transpose(
                         bank[:, r * P : (r + 1) * P], y[:, r, first : first + P], identity[:]
                     )
-                nc.scalar.activation(
-                    out=z_planes[:, t, :],
-                    in_=bank[:],
-                    func=ACT.Identity,
-                    scale=gain_shift[:, c : c + 1],
-                    bias=gain_shift[:, CHUNKS + c : CHUNKS + c + 1],
-                )
+                gain = gain_shift[:, c : c + 1]
+                shift = gain_shift[:, CHUNKS + c : CHUNKS + c + 1]
+                if t % 2 == 0:
+                    nc.vector.tensor_scalar(
+                        out=z_planes[:, t, :], in0=bank[:], scalar1=gain, scalar2=shift, op0=ALU.mult, op1=ALU.add
+                    )
+                else:
+                    nc.scalar.activation(
+                        out=z_planes[:, t, :], in_=bank[:], func=ACT.Identity, scale=gain, bias=shift
+                    )
             z_grouped = z_stage.tile([P, GROUP_ROWS, PACK], BF16, align_bytes=64, name="z_grouped")
-            regroup(nc.vector.tensor_copy, z_planes, z_grouped)
+            regroup(nc.scalar.copy, z_planes, z_grouped)
             return z_grouped
 
         accs_of = {}
@@ -230,21 +235,25 @@ def tile_textguidedcamfusion_pa_kernel(tc, pooled, proto, ln_g, ln_b, W, b, out)
                     stop=(g == PASSES - 1),
                 )
 
-        def finish(s):
-            accs = accs_of[s]
-            square_sum = small.tile([P, GROUP_TILES], F32, name="square_sum")
-            hs = []
+        hs_of = {}
+        inverse_norms = {}
+
+        def add_bias(s):
+            hs_of[s] = []
             for r in range(GROUP_TILES):
                 h = tail.tile([P, D_OUT], F32, name="h", bufs=2 * GROUP_TILES)
-                nc.vector.tensor_tensor(out=h[:], in0=accs[r][:], in1=bias_rows[:], op=ALU.add)
-                hs.append(h)
+                nc.vector.tensor_tensor(out=h[:], in0=accs_of[s][r][:], in1=bias_rows[:], op=ALU.add)
+                hs_of[s].append(h)
+
+        def norms(s):
+            square_sum = small.tile([P, GROUP_TILES], F32, name="square_sum")
             for r in range(GROUP_TILES):
                 squares = tail.tile([P, D_OUT], F32, name="squares", bufs=2)
                 nc.vector.scalar_tensor_tensor(
                     out=squares[:],
-                    in0=hs[r][:],
+                    in0=hs_of[s][r][:],
                     scalar=0.0,
-                    in1=hs[r][:],
+                    in1=hs_of[s][r][:],
                     op0=ALU.max,
                     op1=ALU.mult,
                     accum_out=square_sum[:, r : r + 1],
@@ -253,34 +262,50 @@ def tile_textguidedcamfusion_pa_kernel(tc, pooled, proto, ln_g, ln_b, W, b, out)
             nc.scalar.activation(out=inverse_norm[:], in_=square_sum[:], func=ACT.Sqrt)
             nc.vector.tensor_scalar_max(out=inverse_norm[:], in0=inverse_norm[:], scalar1=TINY_NORM)
             nc.vector.reciprocal(out=inverse_norm[:], in_=inverse_norm[:])
+            inverse_norms[s] = inverse_norm
+
+        def scale_and_store(s):
             for r in range(GROUP_TILES):
                 rt = s * GROUP_TILES + r
+                h = hs_of[s][r]
                 nc.scalar.activation(
-                    out=hs[r][:], in_=hs[r][:], func=ACT.Relu, scale=inverse_norm[:, r : r + 1]
+                    out=h[:], in_=h[:], func=ACT.Relu, scale=inverse_norms[s][:, r : r + 1]
                 )
-                nc.sync.dma_start(out=out[rt * P : (rt + 1) * P, :], in_=hs[r][:])
+                nc.sync.dma_start(out=out[rt * P : (rt + 1) * P, :], in_=h[:])
 
-        row_statistics(0)
-        normalise(0, 0)
+        all_tiles = list(range(GROUP_TILES))
+        for r in all_tiles:
+            tile_statistics(0, r)
+        group_scales(0)
+        for slab in range(SLABS_AHEAD):
+            normalise(0, slab, all_tiles)
         waiting = None
         for s in range(GROUPS):
-            for slab in range(SLABS):
-                if slab + 1 < SLABS:
-                    normalise(s, slab + 1)
-                elif s + 1 < GROUPS:
-                    normalise(s + 1, 0)
-                if slab == 0 and s + 2 < GROUPS:
+            for g in range(PASSES):
+                if g == 0 and s + 2 < GROUPS:
                     load_group(s + 2)
-                if slab == 1 and s + 1 < GROUPS:
-                    row_statistics(s + 1)
-                for g in range(slab * SLAB_PASSES, (slab + 1) * SLAB_PASSES):
-                    z_grouped = flip(s, g)
-                    if s == 0:
-                        quantise_w(g)
-                    if waiting is not None:
-                        multiply(*waiting)
-                    if waiting is not None and g == 0:
-                        finish(s - 1)
-                    waiting = (s, g, z_grouped)
+                z_grouped = flip(s, g)
+                if s == 0:
+                    quantise_w(g)
+                if waiting is not None:
+                    multiply(*waiting)
+                waiting = (s, g, z_grouped)
+                if s > 0 and g == 0:
+                    add_bias(s - 1)
+                if s > 0 and g == 1:
+                    norms(s - 1)
+                if s > 0 and g == 2:
+                    scale_and_store(s - 1)
+                ahead_group, ahead_slab = divmod(s * SLABS + g // SLAB_PASSES + SLABS_AHEAD, SLABS)
+                if ahead_group < GROUPS:
+                    half = GROUP_TILES // SLAB_PASSES
+                    first_tile = (g % SLAB_PASSES) * half
+                    normalise(ahead_group, ahead_slab, all_tiles[first_tile : first_tile + half])
+                if s + 1 < GROUPS and g < GROUP_TILES:
+                    tile_statistics(s + 1, g)
+                if s + 1 < GROUPS and g == GROUP_TILES - 1:
+                    group_scales(s + 1)
         multiply(*waiting)
-        finish(GROUPS - 1)
+        add_bias(GROUPS - 1)
+        norms(GROUPS - 1)
+        scale_and_store(GROUPS - 1)

@@ -32,7 +32,13 @@ STATS_PER_HALF = CHANNELS // STAT_WIDTH
 SLAB = 1024
 SLAB_PASSES = SLAB // K_PASS
 SLABS = FUSED // SLAB
-SLABS_AHEAD = 2
+TOTAL_PASSES = GROUPS * PASSES
+NORMALISE_AHEAD = 4
+REGROUP_LAG = 1
+QUANTISE_LAG = 2
+MULTIPLY_LAG = 3
+NORMS_LAG = 4
+STORE_LAG = 5
 W_AHEAD = 4
 
 FLOPS = 2 * ROWS * FUSED * D_OUT
@@ -174,17 +180,22 @@ def tile_textguidedcamfusion_pa_kernel(tc, pooled, proto, ln_g, ln_b, W, b, out)
             y = y_slabs[(s, slab)]
             for r in row_tiles:
                 if first < CHANNELS:
-                    fused = x_tiles[s * GROUP_TILES + r][:, first : first + SLAB]
+                    nc.vector.tensor_scalar(
+                        out=y[:, r, :],
+                        in0=x_tiles[s * GROUP_TILES + r][:, first : first + SLAB],
+                        scalar1=rstd[:, r : r + 1],
+                        scalar2=shift[:, r : r + 1],
+                        op0=ALU.mult,
+                        op1=ALU.add,
+                    )
                 else:
-                    fused = context[:, first - CHANNELS : first - CHANNELS + SLAB]
-                nc.gpsimd.tensor_scalar(
-                    out=y[:, r, :],
-                    in0=fused,
-                    scalar1=rstd[:, r : r + 1],
-                    scalar2=shift[:, r : r + 1],
-                    op0=ALU.mult,
-                    op1=ALU.add,
-                )
+                    nc.scalar.activation(
+                        out=y[:, r, :],
+                        in_=context[:, first - CHANNELS : first - CHANNELS + SLAB],
+                        func=ACT.Identity,
+                        scale=rstd[:, r : r + 1],
+                        bias=shift[:, r : r + 1],
+                    )
 
         def flip(s, g):
             y = y_slabs[(s, g // SLAB_PASSES)]
@@ -197,32 +208,35 @@ def tile_textguidedcamfusion_pa_kernel(tc, pooled, proto, ln_g, ln_b, W, b, out)
                     nc.tensor.transpose(
                         bank[:, r * P : (r + 1) * P], y[:, r, first : first + P], identity[:]
                     )
-                gain = gain_shift[:, c : c + 1]
-                shift = gain_shift[:, CHUNKS + c : CHUNKS + c + 1]
-                if t % 2 == 0:
-                    nc.vector.tensor_scalar(
-                        out=z_planes[:, t, :], in0=bank[:], scalar1=gain, scalar2=shift, op0=ALU.mult, op1=ALU.add
-                    )
-                else:
-                    nc.scalar.activation(
-                        out=z_planes[:, t, :], in_=bank[:], func=ACT.Identity, scale=gain, bias=shift
-                    )
+                nc.scalar.activation(
+                    out=z_planes[:, t, :],
+                    in_=bank[:],
+                    func=ACT.Identity,
+                    scale=gain_shift[:, c : c + 1],
+                    bias=gain_shift[:, CHUNKS + c : CHUNKS + c + 1],
+                )
+            return z_planes
+
+        def regroup_z(z_planes):
             z_grouped = z_stage.tile([P, GROUP_ROWS, PACK], BF16, align_bytes=64, name="z_grouped")
-            regroup(nc.scalar.copy, z_planes, z_grouped)
+            regroup(nc.vector.tensor_copy, z_planes, z_grouped)
             return z_grouped
+
+        def quantise_z(z_grouped):
+            z_codes = z_words.tile([P, GROUP_ROWS], U32, align_bytes=64, name="z_codes")
+            z_scales = z_words.tile([P, GROUP_ROWS], U8, align_bytes=64, name="z_scales")
+            quantise(nc, z_grouped, z_codes[:], z_scales[:])
+            return z_codes, z_scales
 
         accs_of = {}
 
-        def multiply(s, g, z_grouped):
+        def multiply(s, g, z_codes, z_scales):
             if g == 0:
                 accs_of[s] = []
                 for r in range(GROUP_TILES):
                     acc = acc_psum.tile([P, D_OUT], F32, name="acc")
                     accs_of[s].append(acc)
             accs = accs_of[s]
-            z_codes = z_words.tile([P, GROUP_ROWS], U32, align_bytes=64, name="z_codes")
-            z_scales = z_words.tile([P, GROUP_ROWS], U8, align_bytes=64, name="z_scales")
-            quantise(nc, z_grouped, z_codes[:], z_scales[:])
             for r in range(GROUP_TILES):
                 rows = slice(r * P, (r + 1) * P)
                 nc.tensor.matmul_mx(
@@ -268,44 +282,57 @@ def tile_textguidedcamfusion_pa_kernel(tc, pooled, proto, ln_g, ln_b, W, b, out)
             for r in range(GROUP_TILES):
                 rt = s * GROUP_TILES + r
                 h = hs_of[s][r]
-                nc.scalar.activation(
-                    out=h[:], in_=h[:], func=ACT.Relu, scale=inverse_norms[s][:, r : r + 1]
+                nc.vector.tensor_scalar(
+                    out=h[:],
+                    in0=h[:],
+                    scalar1=0.0,
+                    scalar2=inverse_norms[s][:, r : r + 1],
+                    op0=ALU.max,
+                    op1=ALU.mult,
                 )
                 nc.sync.dma_start(out=out[rt * P : (rt + 1) * P, :], in_=h[:])
 
         all_tiles = list(range(GROUP_TILES))
+        half_tiles = GROUP_TILES // SLAB_PASSES
         for r in all_tiles:
             tile_statistics(0, r)
         group_scales(0)
-        for slab in range(SLABS_AHEAD):
+        for slab in range(NORMALISE_AHEAD // SLAB_PASSES):
             normalise(0, slab, all_tiles)
-        waiting = None
-        for s in range(GROUPS):
-            for g in range(PASSES):
+
+        z_planes_of = {}
+        z_grouped_of = {}
+        z_words_of = {}
+        for step in range(TOTAL_PASSES + STORE_LAG + 1):
+            multiplied = step - MULTIPLY_LAG
+            if 0 <= multiplied < TOTAL_PASSES:
+                s, g = divmod(multiplied, PASSES)
+                multiply(s, g, *z_words_of[multiplied])
+                if g == PASSES - 1:
+                    add_bias(s)
+            if step < TOTAL_PASSES:
+                s, g = divmod(step, PASSES)
                 if g == 0 and s + 2 < GROUPS:
                     load_group(s + 2)
-                z_grouped = flip(s, g)
+                z_planes_of[step] = flip(s, g)
                 if s == 0:
                     quantise_w(g)
-                if waiting is not None:
-                    multiply(*waiting)
-                waiting = (s, g, z_grouped)
-                if s > 0 and g == 0:
-                    add_bias(s - 1)
-                if s > 0 and g == 1:
-                    norms(s - 1)
-                if s > 0 and g == 2:
-                    scale_and_store(s - 1)
-                ahead_group, ahead_slab = divmod(s * SLABS + g // SLAB_PASSES + SLABS_AHEAD, SLABS)
-                if ahead_group < GROUPS:
-                    half = GROUP_TILES // SLAB_PASSES
-                    first_tile = (g % SLAB_PASSES) * half
-                    normalise(ahead_group, ahead_slab, all_tiles[first_tile : first_tile + half])
-                if s + 1 < GROUPS and g < GROUP_TILES:
-                    tile_statistics(s + 1, g)
-                if s + 1 < GROUPS and g == GROUP_TILES - 1:
-                    group_scales(s + 1)
-        multiply(*waiting)
-        add_bias(GROUPS - 1)
-        norms(GROUPS - 1)
-        scale_and_store(GROUPS - 1)
+            if 0 <= step - REGROUP_LAG < TOTAL_PASSES:
+                z_grouped_of[step - REGROUP_LAG] = regroup_z(z_planes_of[step - REGROUP_LAG])
+            if 0 <= step - QUANTISE_LAG < TOTAL_PASSES:
+                z_words_of[step - QUANTISE_LAG] = quantise_z(z_grouped_of[step - QUANTISE_LAG])
+            s, g = divmod(step - NORMS_LAG, PASSES)
+            if 0 <= s < GROUPS and g == PASSES - 1:
+                norms(s)
+            s, g = divmod(step - STORE_LAG, PASSES)
+            if 0 <= s < GROUPS and g == PASSES - 1:
+                scale_and_store(s)
+            if step + NORMALISE_AHEAD < TOTAL_PASSES:
+                s, g = divmod(step + NORMALISE_AHEAD, PASSES)
+                first_tile = (g % SLAB_PASSES) * half_tiles
+                normalise(s, g // SLAB_PASSES, all_tiles[first_tile : first_tile + half_tiles])
+            s, g = divmod(step + PASSES, PASSES)
+            if s < GROUPS and g < GROUP_TILES:
+                tile_statistics(s, g)
+            if s < GROUPS and g == GROUP_TILES - 1:
+                group_scales(s)

from contextlib import ExitStack

import concourse.mybir as mybir
from concourse.masks import make_identity

F32 = mybir.dt.float32
BF16 = mybir.dt.bfloat16
U32 = mybir.dt.uint32
U8 = mybir.dt.uint8
FP8X4 = mybir.dt.float8_e4m3fn_x4
ACT = mybir.ActivationFunctionType
ALU = mybir.AluOpType

P = 128
PACK = 4
K_PASS = P * PACK
ROWS = 2048
CHANNELS = 2048
PROTOS = 64
FUSED = 2 * CHANNELS
D_OUT = 512
EPS = 1e-5
TINY_NORM = 1e-12

PASSES = FUSED // K_PASS
CHUNKS = FUSED // P
GROUP_TILES = 4
GROUP_ROWS = GROUP_TILES * P
GROUPS = ROWS // GROUP_ROWS
STAT_WIDTH = 512
STATS_PER_HALF = CHANNELS // STAT_WIDTH
SLAB = 1024
SLAB_PASSES = SLAB // K_PASS
SLABS = FUSED // SLAB
TOTAL_PASSES = GROUPS * PASSES
NORMALISE_AHEAD = 4
REGROUP_LAG = 1
QUANTISE_LAG = 2
MULTIPLY_LAG = 3
NORMS_LAG = 4
STORE_LAG = 5
W_AHEAD = 4

FLOPS = 2 * ROWS * FUSED * D_OUT


def regroup(copy, planes, grouped):
    copy(
        out=grouped[:].rearrange("p (c i) t -> p c t i", i=4),
        in_=planes[:].rearrange("p t (c i) -> p c t i", i=4),
    )


def quantise(nc, grouped, codes, scales):
    nc.vector.quantize_mx(
        out=codes.bitcast(FP8X4), scales=scales, in_=grouped[:].rearrange("p w t -> p (w t)")
    )


def tile_textguidedcamfusion_pa_kernel(tc, pooled, proto, ln_g, ln_b, W, b, out):
    nc = tc.nc
    with ExitStack() as stack:
        const = stack.enter_context(tc.tile_pool(name="const", bufs=1))
        x_pool = stack.enter_context(tc.tile_pool(name="x", bufs=2 * GROUP_TILES))
        w_stage = stack.enter_context(tc.tile_pool(name="w_stage", bufs=2))
        y_pool = stack.enter_context(tc.tile_pool(name="y", bufs=3))
        z_stage = stack.enter_context(tc.tile_pool(name="z_stage", bufs=3))
        z_words = stack.enter_context(tc.tile_pool(name="z_words", bufs=3))
        small = stack.enter_context(tc.tile_pool(name="small", bufs=2))
        tail = stack.enter_context(tc.tile_pool(name="tail", bufs=GROUP_TILES))
        flip_psum = stack.enter_context(tc.psum_pool(name="flip_psum", bufs=4))
        acc_psum = stack.enter_context(tc.psum_pool(name="acc_psum", bufs=GROUP_TILES))

        x_tiles = {}

        def load_group(s):
            for rt in range(s * GROUP_TILES, (s + 1) * GROUP_TILES):
                x_tile = x_pool.tile([P, CHANNELS], BF16, name="x_tile")
                nc.sync.dma_start(out=x_tile[:], in_=pooled[rt * P : (rt + 1) * P, :])
                x_tiles[rt] = x_tile

        load_group(0)

        gain_shift_rows = const.tile([P, P], BF16)
        nc.vector.memset(gain_shift_rows[:], 0.0)
        nc.scalar.dma_start(out=gain_shift_rows[0:CHUNKS, :], in_=ln_g.rearrange("(c p) -> c p", p=P))
        nc.scalar.dma_start(
            out=gain_shift_rows[CHUNKS : 2 * CHUNKS, :], in_=ln_b.rearrange("(c p) -> c p", p=P)
        )
        proto_rows = const.tile([P, CHANNELS], BF16)
        nc.vector.memset(proto_rows[PROTOS:P, :], 0.0)
        nc.scalar.dma_start(out=proto_rows[0:PROTOS, :], in_=proto)
        bias_rows = const.tile([P, D_OUT], BF16)
        nc.scalar.dma_start(out=bias_rows[:], in_=b.partition_broadcast(P))

        w_view = W.rearrange("(g t p) n -> g p t n", t=PACK, p=P)
        w_planes = {}

        def load_w(g):
            w_plane = w_stage.tile([P, PACK, D_OUT], BF16, name="w_plane", bufs=W_AHEAD)
            nc.sync.dma_start(out=w_plane[:], in_=w_view[g])
            w_planes[g] = w_plane

        for g in range(W_AHEAD):
            load_w(g)
        load_group(1)

        identity = const.tile([P, P], F32)
        make_identity(nc, identity[:])
        ones = const.tile([P, P], BF16)
        nc.vector.memset(ones[:], 1.0)
        eps = const.tile([P, 1], F32)
        nc.vector.memset(eps[:], EPS)

        gain_shift_f32 = const.tile([P, P], F32)
        nc.vector.tensor_copy(out=gain_shift_f32[:], in_=gain_shift_rows[:])
        gain_shift_bank = flip_psum.tile([P, GROUP_ROWS], F32, name="bank")
        nc.tensor.transpose(gain_shift_bank[:, 0:P], gain_shift_f32[:], identity[:])
        gain_shift = const.tile([P, 2 * CHUNKS], F32)
        nc.vector.tensor_copy(out=gain_shift[:], in_=gain_shift_bank[:, 0 : 2 * CHUNKS])

        context = const.tile([P, CHANNELS], F32)
        context_stats = const.tile([P, STATS_PER_HALF, 6], F32)
        for j in range(STATS_PER_HALF):
            cols = slice(j * STAT_WIDTH, (j + 1) * STAT_WIDTH)
            sum_bank = flip_psum.tile([P, GROUP_ROWS], F32, name="bank")
            nc.tensor.matmul(sum_bank[:], lhsT=ones[:], rhs=proto_rows[:, cols], start=True, stop=True)
            nc.scalar.activation(out=context[:, cols], in_=sum_bank[:], func=ACT.Copy, scale=1.0 / PROTOS)
            nc.vector.bn_stats(out=context_stats[:, j, :], in_=context[:, cols])

        stats = const.tile([P, GROUPS * GROUP_TILES, 2 * STATS_PER_HALF, 6], F32)
        nc.vector.tensor_copy(
            out=stats[:, :, STATS_PER_HALF:, :],
            in_=context_stats[:].unsqueeze(1).to_broadcast([P, GROUPS * GROUP_TILES, STATS_PER_HALF, 6]),
        )

        w_codes = const.tile([P, PASSES, D_OUT], U32, align_bytes=64)
        w_scales = const.tile([P, PASSES, D_OUT], U8, align_bytes=64)

        def quantise_w(g):
            w_grouped = w_stage.tile([P, D_OUT, PACK], BF16, align_bytes=64, name="w_grouped")
            regroup(nc.scalar.copy, w_planes[g], w_grouped)
            quantise(nc, w_grouped, w_codes[:, g, :], w_scales[:, g, :])
            if g + W_AHEAD < PASSES:
                load_w(g + W_AHEAD)

        row_scale = {}

        mean_vars = {}

        def tile_statistics(s, r):
            if r == 0:
                mean_vars[s] = small.tile([P, GROUP_TILES, 2], F32, name="mean_var")
            rt = s * GROUP_TILES + r
            for j in range(STATS_PER_HALF):
                cols = slice(j * STAT_WIDTH, (j + 1) * STAT_WIDTH)
                nc.vector.bn_stats(out=stats[:, rt, j, :], in_=x_tiles[rt][:, cols])
            nc.vector.bn_aggr(
                out=mean_vars[s][:, r, :], in_=stats[:, rt, :, :].rearrange("p j v -> p (j v)")
            )

        def group_scales(s):
            mean_var = mean_vars[s]
            rstd = small.tile([P, GROUP_TILES], F32, name="rstd")
            nc.scalar.activation(out=rstd[:], in_=mean_var[:, :, 1], func=ACT.Sqrt, bias=eps[:])
            nc.vector.reciprocal(out=rstd[:], in_=rstd[:])
            shift = small.tile([P, GROUP_TILES], F32, name="shift")
            nc.vector.scalar_tensor_tensor(
                out=shift[:], in0=mean_var[:, :, 0], scalar=-1.0, in1=rstd[:], op0=ALU.mult, op1=ALU.mult
            )
            row_scale[s] = (rstd, shift)

        y_slabs = {}

        def normalise(s, slab, row_tiles):
            rstd, shift = row_scale[s]
            first = slab * SLAB
            if row_tiles[0] == 0:
                y_slabs[(s, slab)] = y_pool.tile([P, GROUP_TILES, SLAB], F32, name="y")
            y = y_slabs[(s, slab)]
            for r in row_tiles:
                if first < CHANNELS:
                    nc.vector.tensor_scalar(
                        out=y[:, r, :],
                        in0=x_tiles[s * GROUP_TILES + r][:, first : first + SLAB],
                        scalar1=rstd[:, r : r + 1],
                        scalar2=shift[:, r : r + 1],
                        op0=ALU.mult,
                        op1=ALU.add,
                    )
                else:
                    nc.scalar.activation(
                        out=y[:, r, :],
                        in_=context[:, first - CHANNELS : first - CHANNELS + SLAB],
                        func=ACT.Identity,
                        scale=rstd[:, r : r + 1],
                        bias=shift[:, r : r + 1],
                    )

        def flip(s, g):
            y = y_slabs[(s, g // SLAB_PASSES)]
            z_planes = z_stage.tile([P, PACK, GROUP_ROWS], BF16, name="z_planes")
            for t in range(PACK):
                c = g * PACK + t
                first = (c * P) % SLAB
                bank = flip_psum.tile([P, GROUP_ROWS], F32, name="bank")
                for r in range(GROUP_TILES):
                    nc.tensor.transpose(
                        bank[:, r * P : (r + 1) * P], y[:, r, first : first + P], identity[:]
                    )
                nc.scalar.activation(
                    out=z_planes[:, t, :],
                    in_=bank[:],
                    func=ACT.Identity,
                    scale=gain_shift[:, c : c + 1],
                    bias=gain_shift[:, CHUNKS + c : CHUNKS + c + 1],
                )
            return z_planes

        def regroup_z(z_planes):
            z_grouped = z_stage.tile([P, GROUP_ROWS, PACK], BF16, align_bytes=64, name="z_grouped")
            regroup(nc.vector.tensor_copy, z_planes, z_grouped)
            return z_grouped

        def quantise_z(z_grouped):
            z_codes = z_words.tile([P, GROUP_ROWS], U32, align_bytes=64, name="z_codes")
            z_scales = z_words.tile([P, GROUP_ROWS], U8, align_bytes=64, name="z_scales")
            quantise(nc, z_grouped, z_codes[:], z_scales[:])
            return z_codes, z_scales

        accs_of = {}

        def multiply(s, g, z_codes, z_scales):
            if g == 0:
                accs_of[s] = []
                for r in range(GROUP_TILES):
                    acc = acc_psum.tile([P, D_OUT], F32, name="acc")
                    accs_of[s].append(acc)
            accs = accs_of[s]
            for r in range(GROUP_TILES):
                rows = slice(r * P, (r + 1) * P)
                nc.tensor.matmul_mx(
                    out=accs[r][:],
                    lhsT=z_codes[:, rows].bitcast(FP8X4),
                    lhsT_scale=z_scales[:, rows],
                    rhs=w_codes[:, g, :].bitcast(FP8X4),
                    rhs_scale=w_scales[:, g, :],
                    start=(g == 0),
                    stop=(g == PASSES - 1),
                )

        hs_of = {}
        inverse_norms = {}

        def add_bias(s):
            hs_of[s] = []
            for r in range(GROUP_TILES):
                h = tail.tile([P, D_OUT], F32, name="h", bufs=2 * GROUP_TILES)
                nc.vector.tensor_tensor(out=h[:], in0=accs_of[s][r][:], in1=bias_rows[:], op=ALU.add)
                hs_of[s].append(h)

        def norms(s):
            square_sum = small.tile([P, GROUP_TILES], F32, name="square_sum")
            for r in range(GROUP_TILES):
                squares = tail.tile([P, D_OUT], F32, name="squares", bufs=2)
                nc.vector.scalar_tensor_tensor(
                    out=squares[:],
                    in0=hs_of[s][r][:],
                    scalar=0.0,
                    in1=hs_of[s][r][:],
                    op0=ALU.max,
                    op1=ALU.mult,
                    accum_out=square_sum[:, r : r + 1],
                )
            inverse_norm = small.tile([P, GROUP_TILES], F32, name="inverse_norm")
            nc.scalar.activation(out=inverse_norm[:], in_=square_sum[:], func=ACT.Sqrt)
            nc.vector.tensor_scalar_max(out=inverse_norm[:], in0=inverse_norm[:], scalar1=TINY_NORM)
            nc.vector.reciprocal(out=inverse_norm[:], in_=inverse_norm[:])
            inverse_norms[s] = inverse_norm

        def scale_and_store(s):
            for r in range(GROUP_TILES):
                rt = s * GROUP_TILES + r
                h = hs_of[s][r]
                nc.vector.tensor_scalar(
                    out=h[:],
                    in0=h[:],
                    scalar1=0.0,
                    scalar2=inverse_norms[s][:, r : r + 1],
                    op0=ALU.max,
                    op1=ALU.mult,
                )
                nc.sync.dma_start(out=out[rt * P : (rt + 1) * P, :], in_=h[:])

        all_tiles = list(range(GROUP_TILES))
        half_tiles = GROUP_TILES // SLAB_PASSES
        for r in all_tiles:
            tile_statistics(0, r)
        group_scales(0)
        for slab in range(NORMALISE_AHEAD // SLAB_PASSES):
            normalise(0, slab, all_tiles)

        z_planes_of = {}
        z_grouped_of = {}
        z_words_of = {}
        for step in range(TOTAL_PASSES + STORE_LAG + 1):
            multiplied = step - MULTIPLY_LAG
            if 0 <= multiplied < TOTAL_PASSES:
                s, g = divmod(multiplied, PASSES)
                multiply(s, g, *z_words_of[multiplied])
                if g == PASSES - 1:
                    add_bias(s)
            if step < TOTAL_PASSES:
                s, g = divmod(step, PASSES)
                if g == 0 and s + 2 < GROUPS:
                    load_group(s + 2)
                z_planes_of[step] = flip(s, g)
                if s == 0:
                    quantise_w(g)
            if 0 <= step - REGROUP_LAG < TOTAL_PASSES:
                z_grouped_of[step - REGROUP_LAG] = regroup_z(z_planes_of[step - REGROUP_LAG])
            if 0 <= step - QUANTISE_LAG < TOTAL_PASSES:
                z_words_of[step - QUANTISE_LAG] = quantise_z(z_grouped_of[step - QUANTISE_LAG])
            s, g = divmod(step - NORMS_LAG, PASSES)
            if 0 <= s < GROUPS and g == PASSES - 1:
                norms(s)
            s, g = divmod(step - STORE_LAG, PASSES)
            if 0 <= s < GROUPS and g == PASSES - 1:
                scale_and_store(s)
            if step + NORMALISE_AHEAD < TOTAL_PASSES:
                s, g = divmod(step + NORMALISE_AHEAD, PASSES)
                first_tile = (g % SLAB_PASSES) * half_tiles
                normalise(s, g // SLAB_PASSES, all_tiles[first_tile : first_tile + half_tiles])
            s, g = divmod(step + PASSES, PASSES)
            if s < GROUPS and g < GROUP_TILES:
                tile_statistics(s, g)
            if s < GROUPS and g == GROUP_TILES - 1:
                group_scales(s)
